import numpy as np
import ml_dtypes


def mxq(x, axis, fmt="e4m3"):
    dtype, down = {"e4m3": (ml_dtypes.float8_e4m3fn, 7), "e5m2": (ml_dtypes.float8_e5m2, 14)}[fmt]
    v = np.moveaxis(np.asarray(x, np.float32).astype(ml_dtypes.bfloat16).astype(np.float64), axis, -1)
    blocks = v.reshape(v.shape[:-1] + (-1, 32))
    amax = np.abs(blocks).max(-1, keepdims=True)
    byte = np.maximum(np.where(amax > 0, np.frexp(amax)[1] - 1 + 127, 0) - down, 1)
    scale = np.exp2(byte - 127.0)
    codes = (blocks / scale).astype(np.float32).astype(dtype).astype(np.float64)
    return np.moveaxis((codes * scale).reshape(v.shape), -1, axis)


WIDE = False


def mx_kscale(k):
    if not WIDE:
        return np.ones(k)
    levels = np.array([10, -10, 5, -5, 0])
    if k % 512:
        return np.exp2(np.random.permutation(np.resize(levels, k // 32))).repeat(32)
    a = np.empty((k // 512, 16))
    for p in range(k // 512):
        a[p, :8] = np.random.permutation(np.resize(levels, 8))
        for g in range(8):
            far = levels[np.abs(levels - a[p, g]) >= 10]
            a[p, g + 8] = far[np.random.randint(len(far))]
    return np.exp2(a.ravel()).repeat(32)


BF16 = ml_dtypes.bfloat16


def bf(x):
    return np.asarray(x, np.float32).astype(BF16)


def f64(x):
    return np.asarray(x).astype(np.float64)


E2M1 = np.array([0.0, 0.5, 1.0, 1.5, 2.0, 3.0, 4.0, 6.0, -0.0, -0.5, -1.0, -1.5, -2.0, -3.0, -4.0, -6.0])


def pack_weight(w, fmt):
    k, n = w.shape
    w = f64(bf(w)).reshape(k // 32, 32, n)
    amax = np.abs(w).max(1)
    if fmt == "e4m3":
        byte = np.frexp(amax)[1] - 1 + 127 - 7
    else:
        mant, ex = np.frexp(amax / 6.0)
        byte = np.where(mant > 0.5, ex, ex - 1) + 127
    byte = np.clip(np.where(amax > 0, byte, 1), 1, 254)
    scaled = (w * np.exp2(127.0 - byte)[:, None, :]).reshape(k, n).astype(np.float32)
    by_word = np.ascontiguousarray(scaled.reshape(k // 512, 128, 4, n).transpose(0, 1, 3, 2))
    if fmt == "e4m3":
        words = by_word.astype(ml_dtypes.float8_e4m3fn).view(np.uint8)
    else:
        c = by_word.astype(ml_dtypes.float4_e2m1fn).view(np.uint8) & 0xF
        words = c[..., 0::2] | (c[..., 1::2] << 4)
    return np.ascontiguousarray(words), np.ascontiguousarray(byte.astype(np.uint8).reshape(k // 512, 16, n))


def unpack_weight(words, scales, fmt):
    g, p, n, _ = words.shape
    if fmt == "e4m3":
        vals = np.ascontiguousarray(words).view(ml_dtypes.float8_e4m3fn).astype(np.float64)
    else:
        nib = np.empty((g, p, n, 4), np.uint8)
        nib[..., 0::2] = words & 0xF
        nib[..., 1::2] = words >> 4
        vals = E2M1[nib]
    vals = vals * np.repeat(np.exp2(scales.astype(np.float64) - 127.0), 8, axis=1)[..., None]
    return vals.transpose(0, 1, 3, 2).reshape(g * 512, n)


B, S, D_IN, MID, FFN, D_OUT, R = 8, 1024, 256, 512, 512, 256, 16
LN_EPS = 1e-5


def silu(v):
    return v / (1.0 + np.exp(-v))


def layer_norm(x, gamma, beta):
    m = np.mean(x, axis=-1, keepdims=True)
    v = np.mean(np.square(x - m), axis=-1, keepdims=True)
    return (x - m) / np.sqrt(v + LN_EPS) * gamma + beta


def draw0():
    t, s = mx_kscale(FFN), mx_kscale(MID)
    h = bf(silu(np.random.standard_normal((B, S, FFN))) * t)
    w_f2_words, w_f2_scales = pack_weight((np.random.standard_normal((MID, FFN)) / np.sqrt(FFN) / t).T, "e4m3")
    b_f2 = bf(0.1 * np.random.standard_normal(MID))
    res1 = bf(0.7 * np.random.standard_normal((B, S, MID)))
    g2 = bf((1.0 + 0.1 * np.random.standard_normal(MID)) * s)
    be2 = bf(0.1 * np.random.standard_normal(MID) * s)
    w_h_words, w_h_scales = pack_weight((np.random.standard_normal((D_OUT, MID)) / np.sqrt(MID) / s).T, "e4m3")
    b_h = bf(0.1 * np.random.standard_normal(D_OUT))
    return {"h": h,
            "w_f2_words": w_f2_words,
            "w_f2_scales": w_f2_scales,
            "b_f2": b_f2,
            "res1": res1,
            "g2": g2,
            "be2": be2,
            "w_h_words": w_h_words,
            "w_h_scales": w_h_scales,
            "b_h": b_h}


def core(h, w_f2_words, w_f2_scales, b_f2, res1, g2, be2, w_h_words, w_h_scales, b_h):
    ffn = (mxq(f64(h), 2, "e4m3") @ unpack_weight(w_f2_words, w_f2_scales, "e4m3")) + f64(b_f2)
    res2 = f64(res1) + ffn
    norm2 = layer_norm(res2, f64(g2), f64(be2))
    return (mxq(norm2, 2, "e4m3") @ unpack_weight(w_h_words, w_h_scales, "e4m3")) + f64(b_h)


def e4m3fn_bytes(y):
    return np.clip(np.asarray(y, np.float64), -448.0, 448.0).astype(np.float32).astype(ml_dtypes.float8_e4m3fn).view(np.uint8)


def e4m3fn_values(b):
    return np.asarray(b, np.uint8).view(ml_dtypes.float8_e4m3fn).astype(np.float64)


def setup_inputs():
    d = draw0()
    x0 = np.asarray(d['h']).astype(np.float64)
    s = (np.max(np.abs(x0), axis=(0, 1), keepdims=True) / 448.0).astype(np.float32)
    out = {}
    for k, v in d.items():
        if k == 'h':
            out['h_bytes'] = e4m3fn_bytes(x0 / s.astype(np.float64))
            out['h_scale'] = s
        else:
            out[k] = v
    return out


def reference(h_bytes, h_scale, w_f2_words, w_f2_scales, b_f2, res1, g2, be2, w_h_words, w_h_scales, b_h):
    return core(e4m3fn_values(h_bytes) * h_scale.astype(np.float64), w_f2_words, w_f2_scales, b_f2, res1, g2, be2, w_h_words, w_h_scales, b_h)

@@ -1,0 +1,306 @@
+from contextlib import ExitStack
+
+import concourse.mybir as mybir
+from concourse.masks import make_identity
+
+B, S, D_IN, MID, D_OUT = 8, 1024, 512, 512, 256
+TOKENS = B * S
+FLOPS = 2 * TOKENS * D_IN * MID + 2 * TOKENS * MID * D_OUT
+EPS = 1e-5
+
+F32 = mybir.dt.float32
+BF16 = mybir.dt.bfloat16
+U32 = mybir.dt.uint32
+I32 = mybir.dt.int32
+U8 = mybir.dt.uint8
+FP8 = mybir.dt.float8_e4m3fn
+FP8X4 = mybir.dt.float8_e4m3fn_x4
+ALU = mybir.AluOpType
+ACT = mybir.ActivationFunctionType
+
+P = 128
+T = 4
+J = 4
+G_TOK = P * J
+GROUPS = TOKENS // G_TOK
+ZENG = "VVVV"
+V_TOK = 384
+
+
+def tile_tsh_mid_block_pb_t_w8_kernel(
+    tc, h_bytes, h_scale, w_f2_words, w_f2_scales, b_f2, res1, g2, be2, w_h_words, w_h_scales, b_h, out
+):
+    nc = tc.nc
+    h_v = h_bytes.rearrange("b s k -> (b s) k").rearrange("(g p j) k -> g p j k", p=P, j=J)
+    res_v = res1.rearrange("b s k -> (b s) k").rearrange("(g p j) k -> g p j k", p=P, j=J)
+    out_v = out.rearrange("b s k -> (b s) k").rearrange("(g p j) k -> g p j k", p=P, j=J)
+
+    with ExitStack() as ctx:
+        keep = ctx.enter_context(tc.tile_pool(name="keep", bufs=1))
+        work = ctx.enter_context(tc.tile_pool(name="work", bufs=2))
+        psum = ctx.enter_context(tc.psum_pool(name="psum", bufs=1))
+        ctx.enter_context(tc.manual_schedule())
+
+        state = {}
+
+        def load_h(g):
+            h_u8 = work.tile([P, J, D_IN], U8, name="h_u8", bufs=4)
+            if g == 0:
+                for i in range(2):
+                    nc.sync.dma_start(out=h_u8[:, 2 * i : 2 * i + 2, :], in_=h_v[g][:, 2 * i : 2 * i + 2, :])
+            else:
+                nc.sync.dma_start(out=h_u8[:], in_=h_v[g])
+            state["h", g] = h_u8
+
+        def load_res(g):
+            res = work.tile([P, J, MID], BF16, name="res", bufs=4)
+            nc.sync.dma_start(out=res[:], in_=res_v[g])
+            state["res", g] = res
+
+        hs = keep.tile([P, 2, D_IN], F32, name="hs")
+        nc.sync.dma_start(out=hs[:, 0, :], in_=h_scale.rearrange("a b k -> (a b k)").partition_broadcast(P))
+        nc.vector.tensor_copy(out=hs[:, 1, :], in_=hs[:, 0, :])
+        load_h(0)
+        w2_raw = keep.tile([P, MID], I32, name="w2_raw", align_bytes=64)
+        nc.sync.dma_start(out=w2_raw[:], in_=w_f2_words[0].rearrange("p n t -> p (n t)").bitcast(I32))
+        w2s_raw = keep.tile([P, MID], U8, name="w2s_raw", align_bytes=64)
+        wh_s = keep.tile([P, D_OUT], U8, name="wh_s", align_bytes=64)
+        nc.gpsimd.memset(w2s_raw[:].bitcast(I32), 0)
+        nc.gpsimd.memset(wh_s[:].bitcast(I32), 0)
+        for r in range(4):
+            nc.sync.dma_start(out=w2s_raw[r:P:32, :].bitcast(I32), in_=w_f2_scales[0, r:16:4, :].bitcast(I32))
+        load_h(1)
+        load_res(0)
+        ident = keep.tile([P, P], F32, name="ident")
+        make_identity(nc, ident[:])
+        w2 = keep.tile([P, MID], I32, name="w2", align_bytes=64)
+        nc.gpsimd.tensor_copy(out=w2[:].rearrange("p (t m) -> p t m", t=T), in_=w2_raw[:].rearrange("p (m t) -> p t m", t=T))
+        w2s = keep.tile([P, MID], U8, name="w2s", align_bytes=64)
+        nc.gpsimd.tensor_copy(out=w2s[:].rearrange("p (t m) -> p m t", t=T), in_=w2s_raw[:].rearrange("p (m t) -> p m t", t=T))
+
+        col = []
+        for name, vec in (("b2", b_f2), ("gain", g2), ("shift", be2)):
+            c_bf = keep.tile([P, T], BF16, name=name + "_bf")
+            nc.sync.dma_start(out=c_bf[:], in_=vec.rearrange("(p t) -> p t", t=T))
+            c = keep.tile([P, T], F32, name=name)
+            nc.gpsimd.tensor_copy(out=c[:], in_=c_bf[:])
+            col.append(c)
+        b2c, gain, shift = col
+
+        wh = keep.tile([P, D_OUT], I32, name="wh", align_bytes=64)
+        bh_bf = keep.tile([P, D_OUT], BF16, name="bh_bf")
+        bh = keep.tile([P, 2, D_OUT], F32, name="bh")
+
+        def late_constants():
+            nc.sync.dma_start(out=wh[:], in_=w_h_words[0].rearrange("p n t -> p (n t)").bitcast(I32))
+            for r in range(4):
+                nc.sync.dma_start(out=wh_s[r:P:32, :].bitcast(I32), in_=w_h_scales[0, r:16:4, :].bitcast(I32))
+            nc.sync.dma_start(out=bh_bf[:], in_=b_h.partition_broadcast(P))
+            for i in range(2):
+                nc.gpsimd.tensor_copy(out=bh[:, i, :], in_=bh_bf[:])
+
+        def hp(g, i):
+            if i == 0:
+                state["hb", g] = work.tile([P, J, D_IN], BF16, name="hb")
+            nc.vector.tensor_tensor(
+                out=state["hb", g][:, 2 * i : 2 * i + 2, :],
+                in0=state["h", g][:, 2 * i : 2 * i + 2, :].bitcast(FP8),
+                in1=hs[:],
+                op=ALU.mult,
+            )
+
+        def ht(g, i):
+            bank = psum.tile([P, 2, 2, P], F32, name="ht", bufs=1)
+            for jj in range(2):
+                words = state["hb", g][:, 2 * i + jj, :].bitcast(F32)
+                for u in range(2):
+                    nc.tensor.transpose(bank[:, jj, u, :], words[:, u : D_IN // 2 : 2], ident[:])
+            state["ht", g, i] = bank
+
+        def hc(g, i):
+            if i == 0:
+                state["hgr", g] = work.tile([P, J, 2 * P, 2], BF16, name="hgr", align_bytes=64)
+            half = state["hgr", g][:, 2 * i : 2 * i + 2].rearrange("p j w e -> p j (w e)").bitcast(F32)
+            nc.scalar.copy(out=half.rearrange("p j (r u) -> p j r u", u=2), in_=state["ht", g, i][:].rearrange("p j u r -> p j r u"))
+
+        def hq(g, i):
+            codes = work.tile([P, G_TOK], U32, name="hq", align_bytes=64)
+            scales = work.tile([P, G_TOK], U8, name="hqs", align_bytes=64)
+            nc.vector.quantize_mx(out=codes[:].bitcast(FP8X4), scales=scales[:], in_=state["hgr", g][:].rearrange("p j w e -> p (j w e)"))
+            state["hq", g] = (codes, scales)
+
+        def mm1(g, t):
+            codes, scales = state["hq", g]
+            acc = psum.tile([P, G_TOK], F32, name="acc", bufs=2)
+            nc.tensor.matmul_mx(
+                out=acc[:],
+                lhsT=w2[:, t * P : (t + 1) * P].bitcast(FP8X4),
+                lhsT_scale=w2s[:, t * P : (t + 1) * P],
+                rhs=codes[:].bitcast(FP8X4),
+                rhs_scale=scales[:],
+                start=True,
+                stop=True,
+            )
+            state["acc", g, t] = acc
+
+        def ff(g, t):
+            if t == 0:
+                state["fT", g] = work.tile([P, T, G_TOK], F32, name="fT")
+            nc.scalar.activation(out=state["fT", g][:, t, :], in_=state["acc", g, t][:], func=ACT.Identity, bias=b2c[:, t : t + 1], scale=1.0)
+
+        def yt(g, j):
+            bank = psum.tile([P, T, P], F32, name="yt", bufs=2)
+            for t in range(T):
+                nc.tensor.transpose(bank[:, t, :], state["fT", g][:, t, j * P : (j + 1) * P], ident[:])
+            state["yt", g, j] = bank
+
+        def t1(g, j):
+            if j == 0:
+                state["y", g] = work.tile([P, J, T, P], F32, name="y", bufs=3)
+                state["sums", g] = work.tile([P, J], F32, name="sums", bufs=3)
+                state["negm", g] = work.tile([P, J], F32, name="negm", bufs=3)
+                state["ss", g] = work.tile([P, J], F32, name="ss", bufs=3)
+                state["rstd", g] = work.tile([P, J], F32, name="rstd", bufs=3)
+                state["nmr", g] = work.tile([P, J], F32, name="nmr", bufs=3)
+                state["z", g] = work.tile([P, J, T, P], F32, name="z")
+            nc.vector.scalar_tensor_tensor(
+                out=state["y", g][:, j],
+                in0=state["yt", g, j][:],
+                scalar=1.0,
+                in1=state["res", g][:, j, :].rearrange("p (m t) -> p t m", t=T),
+                op0=ALU.mult,
+                op1=ALU.add,
+                accum_out=state["sums", g][:, j : j + 1],
+            )
+
+        def negm(g, i):
+            nc.gpsimd.tensor_scalar(out=state["negm", g][:], in0=state["sums", g][:], scalar1=-1.0 / MID, scalar2=0.0, op0=ALU.mult, op1=ALU.add)
+
+        def yrow(g, j):
+            return state["y", g][:, j].rearrange("p t m -> p (t m)")
+
+        def sq(g, j):
+            junk = work.tile([P, MID], BF16, name="junk")
+            nc.scalar.activation(
+                out=junk[:], in_=yrow(g, j), func=ACT.Square, bias=state["sums", g][:, j : j + 1], scale=-float(MID),
+                accum_out=state["ss", g][:, j : j + 1],
+            )
+
+        def rs(g, i):
+            nc.scalar.activation(out=state["rstd", g][:], in_=state["ss", g][:], func=ACT.Abs_reciprocal_sqrt, scale=1.0 / MID**3, bias=EPS)
+
+        def z(g, j):
+            zj = state["z", g][:, j].rearrange("p t m -> p (t m)")
+            s1, s2 = state["negm", g][:, j : j + 1], state["rstd", g][:, j : j + 1]
+            eng = nc.gpsimd if ZENG[j] == "G" else nc.vector
+            eng.tensor_scalar(out=zj, in0=yrow(g, j), scalar1=s1, scalar2=s2, op0=ALU.add, op1=ALU.mult)
+
+        def zt(g, t):
+            bank = psum.tile([P, J, P], F32, name="zt", bufs=2)
+            for j in range(J):
+                nc.tensor.transpose(bank[:, j, :], state["z", g][:, j, t, :], ident[:])
+            state["zt", g, t] = bank
+
+        def aff(g, t):
+            if t == 0:
+                state["pl", g] = work.tile([P, T, G_TOK], BF16, name="pl")
+            nc.scalar.activation(
+                out=state["pl", g][:, t, :], in_=state["zt", g, t][:].rearrange("p j m -> p (j m)"), func=ACT.Identity,
+                scale=gain[:, t : t + 1], bias=shift[:, t : t + 1],
+            )
+
+        def inter(g, i):
+            if i == 0:
+                state["ngr", g] = work.tile([P, G_TOK, T], BF16, name="ngr", align_bytes=64)
+            cols = slice(0, V_TOK) if i == 0 else slice(V_TOK, G_TOK)
+            copy = nc.vector.tensor_copy if i == 0 else nc.scalar.copy
+            copy(out=state["ngr", g][:, cols, :], in_=state["pl", g][:, :, cols].rearrange("p t n -> p n t"))
+
+        def nq(g, i):
+            codes = work.tile([P, G_TOK], U32, name="nq", align_bytes=64)
+            scales = work.tile([P, G_TOK], U8, name="nqs", align_bytes=64)
+            nc.vector.quantize_mx(out=codes[:].bitcast(FP8X4), scales=scales[:], in_=state["ngr", g][:].rearrange("p n t -> p (n t)"))
+            state["nq", g] = (codes, scales)
+
+        def mm2(g, i):
+            codes, scales = state["nq", g]
+            po = psum.tile([P, 2, D_OUT], F32, name="po", bufs=1)
+            for jj in range(2):
+                tok = slice((2 * i + jj) * P, (2 * i + jj + 1) * P)
+                nc.tensor.matmul_mx(
+                    out=po[:, jj, :],
+                    lhsT=codes[:, tok].bitcast(FP8X4),
+                    lhsT_scale=scales[:, tok],
+                    rhs=wh[:].bitcast(FP8X4),
+                    rhs_scale=wh_s[:],
+                    start=True,
+                    stop=True,
+                )
+            state["po", g, i] = po
+
+        def ob(g, i):
+            if i == 0:
+                state["o", g] = work.tile([P, J, D_OUT], F32, name="o")
+            nc.vector.tensor_tensor(out=state["o", g][:, 2 * i : 2 * i + 2, :], in0=state["po", g, i][:], in1=bh[:], op=ALU.add)
+            if i == 1:
+                nc.sync.dma_start(out=out_v[g], in_=state["o", g][:])
+
+        def do(fn, g, *args):
+            if 0 <= g < GROUPS:
+                fn(g, *args)
+
+        for s in range(-5, GROUPS + 6):
+            if s - (-5) + 2 >= 2:
+                do(load_h, s - (-5) + 2)
+            if s - (-1) + 2 >= 1:
+                do(load_res, s - (-1) + 2)
+            if s == -5 + 1:
+                late_constants()
+            do(sq, s - 1, 2)
+            do(mm1, s + 1, 2)
+            do(mm2, s - 6, 1)
+            do(ob, s - 6, 0)
+            do(ht, s + 3, 1)
+            do(z, s - 2, 0)
+            do(aff, s - 3, 0)
+            do(zt, s - 3, 2)
+            do(yt, s - 0, 2)
+            do(z, s - 2, 1)
+            do(z, s - 2, 2)
+            do(mm1, s + 1, 3)
+            do(inter, s - 4, 0)
+            do(t1, s - 0, 1)
+            do(ob, s - 6, 1)
+            do(sq, s - 0, 0)
+            do(ff, s + 1, 2)
+            do(mm1, s + 2, 0)
+            do(t1, s - 0, 2)
+            do(yt, s - 0, 3)
+            do(aff, s - 3, 1)
+            do(z, s - 2, 3)
+            do(hp, s + 4, 1)
+            do(hc, s + 3, 1)
+            do(inter, s - 4, 1)
+            do(ff, s + 1, 3)
+            do(ht, s + 4, 0)
+            do(sq, s - 1, 3)
+            do(hq, s + 3, 0)
+            do(zt, s - 3, 3)
+            do(rs, s - 1, 0)
+            do(t1, s - 0, 3)
+            do(yt, s + 1, 0)
+            do(sq, s - 0, 1)
+            do(mm2, s - 5, 0)
+            do(aff, s - 3, 2)
+            do(mm1, s + 2, 1)
+            do(nq, s - 4, 0)
+            do(zt, s - 2, 0)
+            do(t1, s + 1, 0)
+            do(yt, s + 1, 1)
+            do(ff, s + 2, 0)
+            do(hc, s + 4, 0)
+            do(aff, s - 3, 3)
+            do(ff, s + 2, 1)
+            do(negm, s - 1, 0)
+            do(zt, s - 2, 1)
+            do(hp, s + 5, 0)

@@ -111,6 +111,7 @@ def tile_tsh_mid_block_pb_t_w8_kernel(
 
         def ht(g, i):
             bank = psum.tile([P, 2, 2, P], F32, name="ht", bufs=1)
+            flush(bank[:].rearrange("p j u r -> p (j u r)"))
             for jj in range(2):
                 words = state["hb", g][:, 2 * i + jj, :].bitcast(F32)
                 for u in range(2):
@@ -132,6 +133,7 @@ def tile_tsh_mid_block_pb_t_w8_kernel(
         def mm1(g, t):
             codes, scales = state["hq", g]
             acc = psum.tile([P, G_TOK], F32, name="acc", bufs=2)
+            flush(acc[:])
             nc.tensor.matmul_mx(
                 out=acc[:],
                 lhsT=w2[:, t * P : (t + 1) * P].bitcast(FP8X4),
@@ -150,6 +152,7 @@ def tile_tsh_mid_block_pb_t_w8_kernel(
 
         def yt(g, j):
             bank = psum.tile([P, T, P], F32, name="yt", bufs=2)
+            flush(bank[:].rearrange("p t m -> p (t m)"))
             for t in range(T):
                 nc.tensor.transpose(bank[:, t, :], state["fT", g][:, t, j * P : (j + 1) * P], ident[:])
             state["yt", g, j] = bank
@@ -197,6 +200,7 @@ def tile_tsh_mid_block_pb_t_w8_kernel(
 
         def zt(g, t):
             bank = psum.tile([P, J, P], F32, name="zt", bufs=2)
+            flush(bank[:].rearrange("p j m -> p (j m)"))
             for j in range(J):
                 nc.tensor.transpose(bank[:, j, :], state["z", g][:, j, t, :], ident[:])
             state["zt", g, t] = bank
@@ -225,6 +229,7 @@ def tile_tsh_mid_block_pb_t_w8_kernel(
         def mm2(g, i):
             codes, scales = state["nq", g]
             po = psum.tile([P, 2, D_OUT], F32, name="po", bufs=1)
+            flush(po[:].rearrange("p i n -> p (i n)"), 1)
             for jj in range(2):
                 tok = slice((2 * i + jj) * P, (2 * i + jj + 1) * P)
                 nc.tensor.matmul_mx(
@@ -245,62 +250,85 @@ def tile_tsh_mid_block_pb_t_w8_kernel(
             if i == 1:
                 nc.sync.dma_start(out=out_v[g], in_=state["o", g][:])
 
+        pending = [0]
+
+        def warm(view, n):
+            for i in range(n):
+                nc.tensor.matmul_mx(
+                    out=view,
+                    lhsT=w2_raw[:, 0:P].bitcast(FP8X4),
+                    lhsT_scale=w2s_raw[:, 0:P],
+                    rhs=w2_raw[:].bitcast(FP8X4),
+                    rhs_scale=w2s_raw[:],
+                    start=True,
+                    stop=True,
+                )
+
+        def flush(view, n=0):
+            warm(view, n + pending[0])
+            pending[0] = 0
+
+        def dd(g, i):
+            pending[0] += 2
+
         def do(fn, g, *args):
             if 0 <= g < GROUPS:
                 fn(g, *args)
 
-        for s in range(-5, GROUPS + 6):
-            if s - (-5) + 2 >= 2:
-                do(load_h, s - (-5) + 2)
+        for s in range(-4, GROUPS + 6):
+            if s - (-4) + 2 >= 2:
+                do(load_h, s - (-4) + 2)
             if s - (-1) + 2 >= 1:
                 do(load_res, s - (-1) + 2)
-            if s == -5 + 1:
+            if s == -4 + 1:
                 late_constants()
-            do(sq, s - 1, 2)
-            do(mm1, s + 1, 2)
-            do(mm2, s - 6, 1)
-            do(ob, s - 6, 0)
-            do(ht, s + 3, 1)
             do(z, s - 2, 0)
-            do(aff, s - 3, 0)
-            do(zt, s - 3, 2)
-            do(yt, s - 0, 2)
             do(z, s - 2, 1)
-            do(z, s - 2, 2)
-            do(mm1, s + 1, 3)
-            do(inter, s - 4, 0)
-            do(t1, s - 0, 1)
             do(ob, s - 6, 1)
+            do(zt, s - 3, 2)
+            do(ht, s + 3, 1)
+            do(hp, s + 4, 0)
+            do(mm2, s - 5, 0)
+            do(z, s - 2, 2)
             do(sq, s - 0, 0)
-            do(ff, s + 1, 2)
-            do(mm1, s + 2, 0)
             do(t1, s - 0, 2)
+            do(inter, s - 4, 0)
+            do(inter, s - 4, 1)
             do(yt, s - 0, 3)
+            do(ff, s + 1, 2)
+            do(zt, s - 3, 3)
             do(aff, s - 3, 1)
-            do(z, s - 2, 3)
+            do(t1, s - 0, 3)
+            do(ff, s + 1, 3)
             do(hp, s + 4, 1)
             do(hc, s + 3, 1)
-            do(inter, s - 4, 1)
-            do(ff, s + 1, 3)
-            do(ht, s + 4, 0)
-            do(sq, s - 1, 3)
-            do(hq, s + 3, 0)
-            do(zt, s - 3, 3)
-            do(rs, s - 1, 0)
-            do(t1, s - 0, 3)
-            do(yt, s + 1, 0)
-            do(sq, s - 0, 1)
-            do(mm2, s - 5, 0)
-            do(aff, s - 3, 2)
+            do(z, s - 2, 3)
+            do(mm1, s + 2, 0)
             do(mm1, s + 2, 1)
-            do(nq, s - 4, 0)
-            do(zt, s - 2, 0)
-            do(t1, s + 1, 0)
-            do(yt, s + 1, 1)
+            do(aff, s - 3, 2)
+            do(yt, s + 1, 0)
+            do(ht, s + 4, 0)
+            do(ob, s - 5, 0)
+            do(sq, s - 1, 3)
+            do(dd, s - 0, 0)
             do(ff, s + 2, 0)
-            do(hc, s + 4, 0)
-            do(aff, s - 3, 3)
-            do(ff, s + 2, 1)
+            do(nq, s - 4, 0)
             do(negm, s - 1, 0)
+            do(yt, s + 1, 1)
+            do(zt, s - 2, 0)
+            do(rs, s - 1, 0)
+            do(hq, s + 3, 0)
+            do(ff, s + 2, 1)
+            do(mm1, s + 2, 2)
+            do(t1, s + 1, 0)
+            do(aff, s - 3, 3)
+            do(sq, s - 0, 1)
+            do(t1, s + 1, 1)
+            do(mm2, s - 5, 1)
+            do(mm1, s + 2, 3)
+            do(yt, s + 1, 2)
+            do(sq, s - 0, 2)
+            do(aff, s - 2, 0)
+            do(hc, s + 4, 0)
+            do(dd, s - 0, 1)
             do(zt, s - 2, 1)
-            do(hp, s + 5, 0)

@@ -23,8 +23,8 @@ T = 4
 J = 4
 G_TOK = P * J
 GROUPS = TOKENS // G_TOK
-ZENG = "VVVV"
-V_TOK = 384
+ZENG = "GGGG"
+V_TOK = 512
 
 
 def tile_tsh_mid_block_pb_t_w8_kernel(
@@ -57,7 +57,7 @@ def tile_tsh_mid_block_pb_t_w8_kernel(
             nc.sync.dma_start(out=res[:], in_=res_v[g])
             state["res", g] = res
 
-        hs = keep.tile([P, 2, D_IN], F32, name="hs")
+        hs = keep.tile([P, J, D_IN], F32, name="hs")
         nc.sync.dma_start(out=hs[:, 0, :], in_=h_scale.rearrange("a b k -> (a b k)").partition_broadcast(P))
         nc.vector.tensor_copy(out=hs[:, 1, :], in_=hs[:, 0, :])
         load_h(0)
@@ -100,17 +100,18 @@ def tile_tsh_mid_block_pb_t_w8_kernel(
                 nc.gpsimd.tensor_copy(out=bh[:, i, :], in_=bh_bf[:])
 
         def hp(g, i):
-            if i == 0:
-                state["hb", g] = work.tile([P, J, D_IN], BF16, name="hb")
-            nc.vector.tensor_tensor(
-                out=state["hb", g][:, 2 * i : 2 * i + 2, :],
-                in0=state["h", g][:, 2 * i : 2 * i + 2, :].bitcast(FP8),
-                in1=hs[:],
-                op=ALU.mult,
-            )
+            hb = work.tile([P, J, D_IN], BF16, name="hb")
+            state["hb", g] = hb
+            parts = 2 if g == 0 else 1
+            w = J // parts
+            for q in range(parts):
+                js = slice(q * w, (q + 1) * w)
+                nc.vector.tensor_tensor(out=hb[:, js, :], in0=state["h", g][:, js, :].bitcast(FP8), in1=hs[:, 0:w, :], op=ALU.mult)
+            if g == 0:
+                nc.vector.tensor_copy(out=hs[:, 2:4, :], in_=hs[:, 0:2, :])
 
         def ht(g, i):
-            bank = psum.tile([P, 2, 2, P], F32, name="ht", bufs=1)
+            bank = psum.tile([P, 2, 2, P], F32, name="sbank", bufs=4)
             flush(bank[:].rearrange("p j u r -> p (j u r)"))
             for jj in range(2):
                 words = state["hb", g][:, 2 * i + jj, :].bitcast(F32)
@@ -132,7 +133,7 @@ def tile_tsh_mid_block_pb_t_w8_kernel(
 
         def mm1(g, t):
             codes, scales = state["hq", g]
-            acc = psum.tile([P, G_TOK], F32, name="acc", bufs=2)
+            acc = psum.tile([P, G_TOK], F32, name="sbank", bufs=4)
             flush(acc[:])
             nc.tensor.matmul_mx(
                 out=acc[:],
@@ -151,7 +152,7 @@ def tile_tsh_mid_block_pb_t_w8_kernel(
             nc.scalar.activation(out=state["fT", g][:, t, :], in_=state["acc", g, t][:], func=ACT.Identity, bias=b2c[:, t : t + 1], scale=1.0)
 
         def yt(g, j):
-            bank = psum.tile([P, T, P], F32, name="yt", bufs=2)
+            bank = psum.tile([P, T, P], F32, name="vbank", bufs=4)
             flush(bank[:].rearrange("p t m -> p (t m)"))
             for t in range(T):
                 nc.tensor.transpose(bank[:, t, :], state["fT", g][:, t, j * P : (j + 1) * P], ident[:])
@@ -159,12 +160,12 @@ def tile_tsh_mid_block_pb_t_w8_kernel(
 
         def t1(g, j):
             if j == 0:
-                state["y", g] = work.tile([P, J, T, P], F32, name="y", bufs=3)
-                state["sums", g] = work.tile([P, J], F32, name="sums", bufs=3)
-                state["negm", g] = work.tile([P, J], F32, name="negm", bufs=3)
-                state["ss", g] = work.tile([P, J], F32, name="ss", bufs=3)
-                state["rstd", g] = work.tile([P, J], F32, name="rstd", bufs=3)
-                state["nmr", g] = work.tile([P, J], F32, name="nmr", bufs=3)
+                state["y", g] = work.tile([P, J, T, P], F32, name="y", bufs=4)
+                state["sums", g] = work.tile([P, J], F32, name="sums", bufs=4)
+                state["negm", g] = work.tile([P, J], F32, name="negm", bufs=4)
+                state["ss", g] = work.tile([P, J], F32, name="ss", bufs=4)
+                state["rstd", g] = work.tile([P, J], F32, name="rstd", bufs=4)
+                state["nmr", g] = work.tile([P, J], F32, name="nmr", bufs=4)
                 state["z", g] = work.tile([P, J, T, P], F32, name="z")
             nc.vector.scalar_tensor_tensor(
                 out=state["y", g][:, j],
@@ -176,8 +177,10 @@ def tile_tsh_mid_block_pb_t_w8_kernel(
                 accum_out=state["sums", g][:, j : j + 1],
             )
 
-        def negm(g, i):
-            nc.gpsimd.tensor_scalar(out=state["negm", g][:], in0=state["sums", g][:], scalar1=-1.0 / MID, scalar2=0.0, op0=ALU.mult, op1=ALU.add)
+        def negm(g, j):
+            nc.gpsimd.tensor_scalar(
+                out=state["negm", g][:, j : j + 1], in0=state["sums", g][:, j : j + 1], scalar1=-1.0 / MID, scalar2=0.0, op0=ALU.mult, op1=ALU.add
+            )
 
         def yrow(g, j):
             return state["y", g][:, j].rearrange("p t m -> p (t m)")
@@ -199,7 +202,7 @@ def tile_tsh_mid_block_pb_t_w8_kernel(
             eng.tensor_scalar(out=zj, in0=yrow(g, j), scalar1=s1, scalar2=s2, op0=ALU.add, op1=ALU.mult)
 
         def zt(g, t):
-            bank = psum.tile([P, J, P], F32, name="zt", bufs=2)
+            bank = psum.tile([P, J, P], F32, name="sbank", bufs=4)
             flush(bank[:].rearrange("p j m -> p (j m)"))
             for j in range(J):
                 nc.tensor.transpose(bank[:, j, :], state["z", g][:, j, t, :], ident[:])
@@ -228,7 +231,7 @@ def tile_tsh_mid_block_pb_t_w8_kernel(
 
         def mm2(g, i):
             codes, scales = state["nq", g]
-            po = psum.tile([P, 2, D_OUT], F32, name="po", bufs=1)
+            po = psum.tile([P, 2, D_OUT], F32, name="vbank", bufs=4)
             flush(po[:].rearrange("p i n -> p (i n)"), 1)
             for jj in range(2):
                 tok = slice((2 * i + jj) * P, (2 * i + jj + 1) * P)
@@ -275,60 +278,61 @@ def tile_tsh_mid_block_pb_t_w8_kernel(
             if 0 <= g < GROUPS:
                 fn(g, *args)
 
-        for s in range(-4, GROUPS + 6):
-            if s - (-4) + 2 >= 2:
-                do(load_h, s - (-4) + 2)
+        for s in range(-5, GROUPS + 5):
+            if s - (-5) + 2 >= 2:
+                do(load_h, s - (-5) + 2)
             if s - (-1) + 2 >= 1:
                 do(load_res, s - (-1) + 2)
-            if s == -4 + 1:
+            if s == -5 + 1:
                 late_constants()
-            do(z, s - 2, 0)
-            do(z, s - 2, 1)
-            do(ob, s - 6, 1)
-            do(zt, s - 3, 2)
-            do(ht, s + 3, 1)
-            do(hp, s + 4, 0)
-            do(mm2, s - 5, 0)
-            do(z, s - 2, 2)
-            do(sq, s - 0, 0)
-            do(t1, s - 0, 2)
-            do(inter, s - 4, 0)
-            do(inter, s - 4, 1)
-            do(yt, s - 0, 3)
-            do(ff, s + 1, 2)
-            do(zt, s - 3, 3)
-            do(aff, s - 3, 1)
-            do(t1, s - 0, 3)
-            do(ff, s + 1, 3)
-            do(hp, s + 4, 1)
-            do(hc, s + 3, 1)
-            do(z, s - 2, 3)
             do(mm1, s + 2, 0)
-            do(mm1, s + 2, 1)
-            do(aff, s - 3, 2)
+            do(zt, s - 3, 2)
             do(yt, s + 1, 0)
-            do(ht, s + 4, 0)
+            do(mm1, s + 2, 1)
+            do(sq, s - 0, 0)
+            do(negm, s - 0, 1)
+            do(t1, s - 0, 2)
+            do(zt, s - 3, 3)
+            do(t1, s - 0, 3)
+            do(hc, s + 3, 0)
             do(ob, s - 5, 0)
-            do(sq, s - 1, 3)
-            do(dd, s - 0, 0)
-            do(ff, s + 2, 0)
-            do(nq, s - 4, 0)
-            do(negm, s - 1, 0)
-            do(yt, s + 1, 1)
-            do(zt, s - 2, 0)
-            do(rs, s - 1, 0)
-            do(hq, s + 3, 0)
-            do(ff, s + 2, 1)
-            do(mm1, s + 2, 2)
-            do(t1, s + 1, 0)
-            do(aff, s - 3, 3)
-            do(sq, s - 0, 1)
-            do(t1, s + 1, 1)
             do(mm2, s - 5, 1)
+            do(rs, s - 1, 0)
+            do(ob, s - 5, 1)
+            do(z, s - 1, 0)
+            do(dd, s - 0, 1)
+            do(aff, s - 3, 1)
+            do(t1, s + 1, 0)
+            do(ht, s + 3, 1)
+            do(yt, s + 1, 1)
+            do(aff, s - 3, 2)
+            do(zt, s - 2, 0)
+            do(mm1, s + 2, 2)
+            do(ff, s + 2, 0)
+            do(z, s - 1, 1)
             do(mm1, s + 2, 3)
             do(yt, s + 1, 2)
-            do(sq, s - 0, 2)
-            do(aff, s - 2, 0)
-            do(hc, s + 4, 0)
-            do(dd, s - 0, 1)
+            do(z, s - 1, 2)
+            do(yt, s + 1, 3)
             do(zt, s - 2, 1)
+            do(sq, s - 0, 1)
+            do(aff, s - 3, 3)
+            do(t1, s + 1, 1)
+            do(ff, s + 2, 1)
+            do(z, s - 1, 3)
+            do(sq, s - 0, 2)
+            do(inter, s - 3, 0)
+            do(hc, s + 3, 1)
+            do(dd, s - 0, 0)
+            do(negm, s - 0, 2)
+            do(ht, s + 4, 0)
+            do(aff, s - 2, 0)
+            do(hq, s + 3, 0)
+            do(negm, s - 0, 3)
+            do(negm, s + 1, 0)
+            do(ff, s + 2, 2)
+            do(hp, s + 5, 0)
+            do(ff, s + 2, 3)
+            do(nq, s - 3, 0)
+            do(mm2, s - 4, 0)
+            do(sq, s - 0, 3)

@@ -23,8 +23,7 @@ T = 4
 J = 4
 G_TOK = P * J
 GROUPS = TOKENS // G_TOK
-ZENG = "GGGG"
-V_TOK = 512
+ZENG = "GGGV"
 
 
 def tile_tsh_mid_block_pb_t_w8_kernel(
@@ -112,7 +111,6 @@ def tile_tsh_mid_block_pb_t_w8_kernel(
 
         def ht(g, i):
             bank = psum.tile([P, 2, 2, P], F32, name="sbank", bufs=4)
-            flush(bank[:].rearrange("p j u r -> p (j u r)"))
             for jj in range(2):
                 words = state["hb", g][:, 2 * i + jj, :].bitcast(F32)
                 for u in range(2):
@@ -123,7 +121,8 @@ def tile_tsh_mid_block_pb_t_w8_kernel(
             if i == 0:
                 state["hgr", g] = work.tile([P, J, 2 * P, 2], BF16, name="hgr", align_bytes=64)
             half = state["hgr", g][:, 2 * i : 2 * i + 2].rearrange("p j w e -> p j (w e)").bitcast(F32)
-            nc.scalar.copy(out=half.rearrange("p j (r u) -> p j r u", u=2), in_=state["ht", g, i][:].rearrange("p j u r -> p j r u"))
+            copy = nc.vector.tensor_copy if (i == 1 and 4 <= g < 8) else nc.scalar.copy
+            copy(out=half.rearrange("p j (r u) -> p j r u", u=2), in_=state["ht", g, i][:].rearrange("p j u r -> p j r u"))
 
         def hq(g, i):
             codes = work.tile([P, G_TOK], U32, name="hq", align_bytes=64)
@@ -134,7 +133,6 @@ def tile_tsh_mid_block_pb_t_w8_kernel(
         def mm1(g, t):
             codes, scales = state["hq", g]
             acc = psum.tile([P, G_TOK], F32, name="sbank", bufs=4)
-            flush(acc[:])
             nc.tensor.matmul_mx(
                 out=acc[:],
                 lhsT=w2[:, t * P : (t + 1) * P].bitcast(FP8X4),
@@ -149,11 +147,13 @@ def tile_tsh_mid_block_pb_t_w8_kernel(
         def ff(g, t):
             if t == 0:
                 state["fT", g] = work.tile([P, T, G_TOK], F32, name="fT")
-            nc.scalar.activation(out=state["fT", g][:, t, :], in_=state["acc", g, t][:], func=ACT.Identity, bias=b2c[:, t : t + 1], scale=1.0)
+            if (t == 0 and 12 <= g < 15):
+                nc.vector.tensor_scalar_add(out=state["fT", g][:, t, :], in0=state["acc", g, t][:], scalar1=b2c[:, t : t + 1])
+            else:
+                nc.scalar.activation(out=state["fT", g][:, t, :], in_=state["acc", g, t][:], func=ACT.Identity, bias=b2c[:, t : t + 1], scale=1.0)
 
         def yt(g, j):
             bank = psum.tile([P, T, P], F32, name="vbank", bufs=4)
-            flush(bank[:].rearrange("p t m -> p (t m)"))
             for t in range(T):
                 nc.tensor.transpose(bank[:, t, :], state["fT", g][:, t, j * P : (j + 1) * P], ident[:])
             state["yt", g, j] = bank
@@ -166,7 +166,6 @@ def tile_tsh_mid_block_pb_t_w8_kernel(
                 state["ss", g] = work.tile([P, J], F32, name="ss", bufs=4)
                 state["rstd", g] = work.tile([P, J], F32, name="rstd", bufs=4)
                 state["nmr", g] = work.tile([P, J], F32, name="nmr", bufs=4)
-                state["z", g] = work.tile([P, J, T, P], F32, name="z")
             nc.vector.scalar_tensor_tensor(
                 out=state["y", g][:, j],
                 in0=state["yt", g, j][:],
@@ -196,6 +195,8 @@ def tile_tsh_mid_block_pb_t_w8_kernel(
             nc.scalar.activation(out=state["rstd", g][:], in_=state["ss", g][:], func=ACT.Abs_reciprocal_sqrt, scale=1.0 / MID**3, bias=EPS)
 
         def z(g, j):
+            if j == 0:
+                state["z", g] = work.tile([P, J, T, P], F32, name="z")
             zj = state["z", g][:, j].rearrange("p t m -> p (t m)")
             s1, s2 = state["negm", g][:, j : j + 1], state["rstd", g][:, j : j + 1]
             eng = nc.gpsimd if ZENG[j] == "G" else nc.vector
@@ -203,7 +204,6 @@ def tile_tsh_mid_block_pb_t_w8_kernel(
 
         def zt(g, t):
             bank = psum.tile([P, J, P], F32, name="sbank", bufs=4)
-            flush(bank[:].rearrange("p j m -> p (j m)"))
             for j in range(J):
                 nc.tensor.transpose(bank[:, j, :], state["z", g][:, j, t, :], ident[:])
             state["zt", g, t] = bank
@@ -216,23 +216,28 @@ def tile_tsh_mid_block_pb_t_w8_kernel(
                 scale=gain[:, t : t + 1], bias=shift[:, t : t + 1],
             )
 
+        def halves(g):
+            n = 2 if g == GROUPS - 1 else 1
+            return [slice(q * G_TOK // n, (q + 1) * G_TOK // n) for q in range(n)]
+
         def inter(g, i):
-            if i == 0:
-                state["ngr", g] = work.tile([P, G_TOK, T], BF16, name="ngr", align_bytes=64)
-            cols = slice(0, V_TOK) if i == 0 else slice(V_TOK, G_TOK)
-            copy = nc.vector.tensor_copy if i == 0 else nc.scalar.copy
-            copy(out=state["ngr", g][:, cols, :], in_=state["pl", g][:, :, cols].rearrange("p t n -> p n t"))
+            ngr = work.tile([P, G_TOK, T], BF16, name="ngr", align_bytes=64)
+            for cols in halves(g):
+                nc.vector.tensor_copy(out=ngr[:, cols, :], in_=state["pl", g][:, :, cols].rearrange("p t n -> p n t"))
+            state["ngr", g] = ngr
 
         def nq(g, i):
             codes = work.tile([P, G_TOK], U32, name="nq", align_bytes=64)
             scales = work.tile([P, G_TOK], U8, name="nqs", align_bytes=64)
-            nc.vector.quantize_mx(out=codes[:].bitcast(FP8X4), scales=scales[:], in_=state["ngr", g][:].rearrange("p n t -> p (n t)"))
+            for cols in halves(g):
+                nc.vector.quantize_mx(
+                    out=codes[:, cols].bitcast(FP8X4), scales=scales[:, cols], in_=state["ngr", g][:, cols, :].rearrange("p n t -> p (n t)")
+                )
             state["nq", g] = (codes, scales)
 
         def mm2(g, i):
             codes, scales = state["nq", g]
             po = psum.tile([P, 2, D_OUT], F32, name="vbank", bufs=4)
-            flush(po[:].rearrange("p i n -> p (i n)"), 1)
             for jj in range(2):
                 tok = slice((2 * i + jj) * P, (2 * i + jj + 1) * P)
                 nc.tensor.matmul_mx(
@@ -250,89 +255,69 @@ def tile_tsh_mid_block_pb_t_w8_kernel(
             if i == 0:
                 state["o", g] = work.tile([P, J, D_OUT], F32, name="o")
             nc.vector.tensor_tensor(out=state["o", g][:, 2 * i : 2 * i + 2, :], in0=state["po", g, i][:], in1=bh[:], op=ALU.add)
-            if i == 1:
+            if g == GROUPS - 1:
+                js = slice(2 * i, 2 * i + 2)
+                nc.sync.dma_start(out=out_v[g][:, js, :], in_=state["o", g][:, js, :])
+            elif i == 1:
                 nc.sync.dma_start(out=out_v[g], in_=state["o", g][:])
-
-        pending = [0]
-
-        def warm(view, n):
-            for i in range(n):
-                nc.tensor.matmul_mx(
-                    out=view,
-                    lhsT=w2_raw[:, 0:P].bitcast(FP8X4),
-                    lhsT_scale=w2s_raw[:, 0:P],
-                    rhs=w2_raw[:].bitcast(FP8X4),
-                    rhs_scale=w2s_raw[:],
-                    start=True,
-                    stop=True,
-                )
-
-        def flush(view, n=0):
-            warm(view, n + pending[0])
-            pending[0] = 0
-
-        def dd(g, i):
-            pending[0] += 2
 
         def do(fn, g, *args):
             if 0 <= g < GROUPS:
                 fn(g, *args)
 
-        for s in range(-5, GROUPS + 5):
-            if s - (-5) + 2 >= 2:
-                do(load_h, s - (-5) + 2)
+        for s in range(-4, GROUPS + 5):
+            if s - (-4) + 2 >= 2:
+                do(load_h, s - (-4) + 2)
             if s - (-1) + 2 >= 1:
                 do(load_res, s - (-1) + 2)
-            if s == -5 + 1:
+            if s == -4 + 1:
                 late_constants()
-            do(mm1, s + 2, 0)
-            do(zt, s - 3, 2)
-            do(yt, s + 1, 0)
-            do(mm1, s + 2, 1)
-            do(sq, s - 0, 0)
-            do(negm, s - 0, 1)
-            do(t1, s - 0, 2)
-            do(zt, s - 3, 3)
-            do(t1, s - 0, 3)
-            do(hc, s + 3, 0)
-            do(ob, s - 5, 0)
-            do(mm2, s - 5, 1)
+            do(inter, s - 4, 0)
             do(rs, s - 1, 0)
-            do(ob, s - 5, 1)
-            do(z, s - 1, 0)
-            do(dd, s - 0, 1)
-            do(aff, s - 3, 1)
-            do(t1, s + 1, 0)
-            do(ht, s + 3, 1)
-            do(yt, s + 1, 1)
+            do(ob, s - 5, 0)
+            do(t1, s - 0, 1)
             do(aff, s - 3, 2)
-            do(zt, s - 2, 0)
+            do(mm1, s + 2, 1)
+            do(yt, s + 1, 0)
             do(mm1, s + 2, 2)
-            do(ff, s + 2, 0)
-            do(z, s - 1, 1)
-            do(mm1, s + 2, 3)
-            do(yt, s + 1, 2)
-            do(z, s - 1, 2)
-            do(yt, s + 1, 3)
-            do(zt, s - 2, 1)
-            do(sq, s - 0, 1)
             do(aff, s - 3, 3)
-            do(t1, s + 1, 1)
-            do(ff, s + 2, 1)
-            do(z, s - 1, 3)
-            do(sq, s - 0, 2)
-            do(inter, s - 3, 0)
-            do(hc, s + 3, 1)
-            do(dd, s - 0, 0)
-            do(negm, s - 0, 2)
-            do(ht, s + 4, 0)
-            do(aff, s - 2, 0)
-            do(hq, s + 3, 0)
-            do(negm, s - 0, 3)
-            do(negm, s + 1, 0)
-            do(ff, s + 2, 2)
-            do(hp, s + 5, 0)
-            do(ff, s + 2, 3)
-            do(nq, s - 3, 0)
+            do(hp, s + 4, 0)
+            do(negm, s - 1, 2)
+            do(nq, s - 4, 0)
+            do(mm1, s + 2, 3)
+            do(sq, s - 0, 0)
             do(mm2, s - 4, 0)
+            do(z, s - 2, 3)
+            do(zt, s - 2, 0)
+            do(negm, s - 1, 3)
+            do(negm, s - 0, 0)
+            do(hc, s + 3, 1)
+            do(sq, s - 0, 1)
+            do(t1, s - 0, 2)
+            do(ff, s + 2, 0)
+            do(zt, s - 2, 1)
+            do(yt, s + 1, 1)
+            do(ff, s + 2, 1)
+            do(ob, s - 5, 1)
+            do(ht, s + 4, 0)
+            do(t1, s - 0, 3)
+            do(zt, s - 2, 2)
+            do(ff, s + 2, 2)
+            do(ht, s + 4, 1)
+            do(yt, s + 1, 2)
+            do(zt, s - 2, 3)
+            do(negm, s - 0, 1)
+            do(yt, s + 1, 3)
+            do(ff, s + 2, 3)
+            do(sq, s - 0, 2)
+            do(aff, s - 2, 0)
+            do(t1, s + 1, 0)
+            do(z, s - 1, 0)
+            do(hq, s + 3, 0)
+            do(z, s - 1, 1)
             do(sq, s - 0, 3)
+            do(aff, s - 2, 1)
+            do(mm2, s - 4, 1)
+            do(mm1, s + 3, 0)
+            do(hc, s + 4, 0)
+            do(z, s - 1, 2)

from contextlib import ExitStack

import concourse.mybir as mybir
from concourse.masks import make_identity

B, S, D_IN, MID, D_OUT = 8, 1024, 512, 512, 256
TOKENS = B * S
FLOPS = 2 * TOKENS * D_IN * MID + 2 * TOKENS * MID * D_OUT
EPS = 1e-5

F32 = mybir.dt.float32
BF16 = mybir.dt.bfloat16
U32 = mybir.dt.uint32
I32 = mybir.dt.int32
U8 = mybir.dt.uint8
FP8 = mybir.dt.float8_e4m3fn
FP8X4 = mybir.dt.float8_e4m3fn_x4
ALU = mybir.AluOpType
ACT = mybir.ActivationFunctionType

P = 128
T = 4
J = 4
G_TOK = P * J
GROUPS = TOKENS // G_TOK
ZENG = "GGGV"


def tile_tsh_mid_block_pb_t_w8_kernel(
    tc, h_bytes, h_scale, w_f2_words, w_f2_scales, b_f2, res1, g2, be2, w_h_words, w_h_scales, b_h, out
):
    nc = tc.nc
    h_v = h_bytes.rearrange("b s k -> (b s) k").rearrange("(g p j) k -> g p j k", p=P, j=J)
    res_v = res1.rearrange("b s k -> (b s) k").rearrange("(g p j) k -> g p j k", p=P, j=J)
    out_v = out.rearrange("b s k -> (b s) k").rearrange("(g p j) k -> g p j k", p=P, j=J)

    with ExitStack() as ctx:
        keep = ctx.enter_context(tc.tile_pool(name="keep", bufs=1))
        work = ctx.enter_context(tc.tile_pool(name="work", bufs=2))
        psum = ctx.enter_context(tc.psum_pool(name="psum", bufs=1))
        ctx.enter_context(tc.manual_schedule())

        state = {}

        def load_h(g):
            h_u8 = work.tile([P, J, D_IN], U8, name="h_u8", bufs=4)
            if g == 0:
                for i in range(2):
                    nc.sync.dma_start(out=h_u8[:, 2 * i : 2 * i + 2, :], in_=h_v[g][:, 2 * i : 2 * i + 2, :])
            else:
                nc.sync.dma_start(out=h_u8[:], in_=h_v[g])
            state["h", g] = h_u8

        def load_res(g):
            res = work.tile([P, J, MID], BF16, name="res", bufs=4)
            nc.sync.dma_start(out=res[:], in_=res_v[g])
            state["res", g] = res

        hs = keep.tile([P, J, D_IN], F32, name="hs")
        nc.sync.dma_start(out=hs[:, 0, :], in_=h_scale.rearrange("a b k -> (a b k)").partition_broadcast(P))
        nc.vector.tensor_copy(out=hs[:, 1, :], in_=hs[:, 0, :])
        load_h(0)
        w2_raw = keep.tile([P, MID], I32, name="w2_raw", align_bytes=64)
        nc.sync.dma_start(out=w2_raw[:], in_=w_f2_words[0].rearrange("p n t -> p (n t)").bitcast(I32))
        w2s_raw = keep.tile([P, MID], U8, name="w2s_raw", align_bytes=64)
        wh_s = keep.tile([P, D_OUT], U8, name="wh_s", align_bytes=64)
        nc.gpsimd.memset(w2s_raw[:].bitcast(I32), 0)
        nc.gpsimd.memset(wh_s[:].bitcast(I32), 0)
        for r in range(4):
            nc.sync.dma_start(out=w2s_raw[r:P:32, :].bitcast(I32), in_=w_f2_scales[0, r:16:4, :].bitcast(I32))
        load_h(1)
        load_res(0)
        ident = keep.tile([P, P], F32, name="ident")
        make_identity(nc, ident[:])
        w2 = keep.tile([P, MID], I32, name="w2", align_bytes=64)
        nc.gpsimd.tensor_copy(out=w2[:].rearrange("p (t m) -> p t m", t=T), in_=w2_raw[:].rearrange("p (m t) -> p t m", t=T))
        w2s = keep.tile([P, MID], U8, name="w2s", align_bytes=64)
        nc.gpsimd.tensor_copy(out=w2s[:].rearrange("p (t m) -> p m t", t=T), in_=w2s_raw[:].rearrange("p (m t) -> p m t", t=T))

        col = []
        for name, vec in (("b2", b_f2), ("gain", g2), ("shift", be2)):
            c_bf = keep.tile([P, T], BF16, name=name + "_bf")
            nc.sync.dma_start(out=c_bf[:], in_=vec.rearrange("(p t) -> p t", t=T))
            c = keep.tile([P, T], F32, name=name)
            nc.gpsimd.tensor_copy(out=c[:], in_=c_bf[:])
            col.append(c)
        b2c, gain, shift = col

        wh = keep.tile([P, D_OUT], I32, name="wh", align_bytes=64)
        bh_bf = keep.tile([P, D_OUT], BF16, name="bh_bf")
        bh = keep.tile([P, 2, D_OUT], F32, name="bh")

        def late_constants():
            nc.sync.dma_start(out=wh[:], in_=w_h_words[0].rearrange("p n t -> p (n t)").bitcast(I32))
            for r in range(4):
                nc.sync.dma_start(out=wh_s[r:P:32, :].bitcast(I32), in_=w_h_scales[0, r:16:4, :].bitcast(I32))
            nc.sync.dma_start(out=bh_bf[:], in_=b_h.partition_broadcast(P))
            for i in range(2):
                nc.gpsimd.tensor_copy(out=bh[:, i, :], in_=bh_bf[:])

        def hp(g, i):
            hb = work.tile([P, J, D_IN], BF16, name="hb")
            state["hb", g] = hb
            parts = 2 if g == 0 else 1
            w = J // parts
            for q in range(parts):
                js = slice(q * w, (q + 1) * w)
                nc.vector.tensor_tensor(out=hb[:, js, :], in0=state["h", g][:, js, :].bitcast(FP8), in1=hs[:, 0:w, :], op=ALU.mult)
            if g == 0:
                nc.vector.tensor_copy(out=hs[:, 2:4, :], in_=hs[:, 0:2, :])

        def ht(g, i):
            bank = psum.tile([P, 2, 2, P], F32, name="sbank", bufs=4)
            for jj in range(2):
                words = state["hb", g][:, 2 * i + jj, :].bitcast(F32)
                for u in range(2):
                    nc.tensor.transpose(bank[:, jj, u, :], words[:, u : D_IN // 2 : 2], ident[:])
            state["ht", g, i] = bank

        def hc(g, i):
            if i == 0:
                state["hgr", g] = work.tile([P, J, 2 * P, 2], BF16, name="hgr", align_bytes=64)
            half = state["hgr", g][:, 2 * i : 2 * i + 2].rearrange("p j w e -> p j (w e)").bitcast(F32)
            copy = nc.vector.tensor_copy if (i == 1 and 4 <= g < 8) else nc.scalar.copy
            copy(out=half.rearrange("p j (r u) -> p j r u", u=2), in_=state["ht", g, i][:].rearrange("p j u r -> p j r u"))

        def hq(g, i):
            codes = work.tile([P, G_TOK], U32, name="hq", align_bytes=64)
            scales = work.tile([P, G_TOK], U8, name="hqs", align_bytes=64)
            nc.vector.quantize_mx(out=codes[:].bitcast(FP8X4), scales=scales[:], in_=state["hgr", g][:].rearrange("p j w e -> p (j w e)"))
            state["hq", g] = (codes, scales)

        def mm1(g, t):
            codes, scales = state["hq", g]
            acc = psum.tile([P, G_TOK], F32, name="sbank", bufs=4)
            nc.tensor.matmul_mx(
                out=acc[:],
                lhsT=w2[:, t * P : (t + 1) * P].bitcast(FP8X4),
                lhsT_scale=w2s[:, t * P : (t + 1) * P],
                rhs=codes[:].bitcast(FP8X4),
                rhs_scale=scales[:],
                start=True,
                stop=True,
            )
            state["acc", g, t] = acc

        def ff(g, t):
            if t == 0:
                state["fT", g] = work.tile([P, T, G_TOK], F32, name="fT")
            if (t == 0 and 12 <= g < 15):
                nc.vector.tensor_scalar_add(out=state["fT", g][:, t, :], in0=state["acc", g, t][:], scalar1=b2c[:, t : t + 1])
            else:
                nc.scalar.activation(out=state["fT", g][:, t, :], in_=state["acc", g, t][:], func=ACT.Identity, bias=b2c[:, t : t + 1], scale=1.0)

        def yt(g, j):
            bank = psum.tile([P, T, P], F32, name="vbank", bufs=4)
            for t in range(T):
                nc.tensor.transpose(bank[:, t, :], state["fT", g][:, t, j * P : (j + 1) * P], ident[:])
            state["yt", g, j] = bank

        def t1(g, j):
            if j == 0:
                state["y", g] = work.tile([P, J, T, P], F32, name="y", bufs=4)
                state["sums", g] = work.tile([P, J], F32, name="sums", bufs=4)
                state["negm", g] = work.tile([P, J], F32, name="negm", bufs=4)
                state["ss", g] = work.tile([P, J], F32, name="ss", bufs=4)
                state["rstd", g] = work.tile([P, J], F32, name="rstd", bufs=4)
                state["nmr", g] = work.tile([P, J], F32, name="nmr", bufs=4)
            nc.vector.scalar_tensor_tensor(
                out=state["y", g][:, j],
                in0=state["yt", g, j][:],
                scalar=1.0,
                in1=state["res", g][:, j, :].rearrange("p (m t) -> p t m", t=T),
                op0=ALU.mult,
                op1=ALU.add,
                accum_out=state["sums", g][:, j : j + 1],
            )

        def negm(g, j):
            nc.gpsimd.tensor_scalar(
                out=state["negm", g][:, j : j + 1], in0=state["sums", g][:, j : j + 1], scalar1=-1.0 / MID, scalar2=0.0, op0=ALU.mult, op1=ALU.add
            )

        def yrow(g, j):
            return state["y", g][:, j].rearrange("p t m -> p (t m)")

        def sq(g, j):
            junk = work.tile([P, MID], BF16, name="junk")
            nc.scalar.activation(
                out=junk[:], in_=yrow(g, j), func=ACT.Square, bias=state["sums", g][:, j : j + 1], scale=-float(MID),
                accum_out=state["ss", g][:, j : j + 1],
            )

        def rs(g, i):
            nc.scalar.activation(out=state["rstd", g][:], in_=state["ss", g][:], func=ACT.Abs_reciprocal_sqrt, scale=1.0 / MID**3, bias=EPS)

        def z(g, j):
            if j == 0:
                state["z", g] = work.tile([P, J, T, P], F32, name="z")
            zj = state["z", g][:, j].rearrange("p t m -> p (t m)")
            s1, s2 = state["negm", g][:, j : j + 1], state["rstd", g][:, j : j + 1]
            eng = nc.gpsimd if ZENG[j] == "G" else nc.vector
            eng.tensor_scalar(out=zj, in0=yrow(g, j), scalar1=s1, scalar2=s2, op0=ALU.add, op1=ALU.mult)

        def zt(g, t):
            bank = psum.tile([P, J, P], F32, name="sbank", bufs=4)
            for j in range(J):
                nc.tensor.transpose(bank[:, j, :], state["z", g][:, j, t, :], ident[:])
            state["zt", g, t] = bank

        def aff(g, t):
            if t == 0:
                state["pl", g] = work.tile([P, T, G_TOK], BF16, name="pl")
            nc.scalar.activation(
                out=state["pl", g][:, t, :], in_=state["zt", g, t][:].rearrange("p j m -> p (j m)"), func=ACT.Identity,
                scale=gain[:, t : t + 1], bias=shift[:, t : t + 1],
            )

        def halves(g):
            n = 2 if g == GROUPS - 1 else 1
            return [slice(q * G_TOK // n, (q + 1) * G_TOK // n) for q in range(n)]

        def inter(g, i):
            ngr = work.tile([P, G_TOK, T], BF16, name="ngr", align_bytes=64)
            for cols in halves(g):
                nc.vector.tensor_copy(out=ngr[:, cols, :], in_=state["pl", g][:, :, cols].rearrange("p t n -> p n t"))
            state["ngr", g] = ngr

        def nq(g, i):
            codes = work.tile([P, G_TOK], U32, name="nq", align_bytes=64)
            scales = work.tile([P, G_TOK], U8, name="nqs", align_bytes=64)
            for cols in halves(g):
                nc.vector.quantize_mx(
                    out=codes[:, cols].bitcast(FP8X4), scales=scales[:, cols], in_=state["ngr", g][:, cols, :].rearrange("p n t -> p (n t)")
                )
            state["nq", g] = (codes, scales)

        def mm2(g, i):
            codes, scales = state["nq", g]
            po = psum.tile([P, 2, D_OUT], F32, name="vbank", bufs=4)
            for jj in range(2):
                tok = slice((2 * i + jj) * P, (2 * i + jj + 1) * P)
                nc.tensor.matmul_mx(
                    out=po[:, jj, :],
                    lhsT=codes[:, tok].bitcast(FP8X4),
                    lhsT_scale=scales[:, tok],
                    rhs=wh[:].bitcast(FP8X4),
                    rhs_scale=wh_s[:],
                    start=True,
                    stop=True,
                )
            state["po", g, i] = po

        def ob(g, i):
            if i == 0:
                state["o", g] = work.tile([P, J, D_OUT], F32, name="o")
            nc.vector.tensor_tensor(out=state["o", g][:, 2 * i : 2 * i + 2, :], in0=state["po", g, i][:], in1=bh[:], op=ALU.add)
            if g == GROUPS - 1:
                js = slice(2 * i, 2 * i + 2)
                nc.sync.dma_start(out=out_v[g][:, js, :], in_=state["o", g][:, js, :])
            elif i == 1:
                nc.sync.dma_start(out=out_v[g], in_=state["o", g][:])

        def do(fn, g, *args):
            if 0 <= g < GROUPS:
                fn(g, *args)

        for s in range(-4, GROUPS + 5):
            if s - (-4) + 2 >= 2:
                do(load_h, s - (-4) + 2)
            if s - (-1) + 2 >= 1:
                do(load_res, s - (-1) + 2)
            if s == -4 + 1:
                late_constants()
            do(inter, s - 4, 0)
            do(rs, s - 1, 0)
            do(ob, s - 5, 0)
            do(t1, s - 0, 1)
            do(aff, s - 3, 2)
            do(mm1, s + 2, 1)
            do(yt, s + 1, 0)
            do(mm1, s + 2, 2)
            do(aff, s - 3, 3)
            do(hp, s + 4, 0)
            do(negm, s - 1, 2)
            do(nq, s - 4, 0)
            do(mm1, s + 2, 3)
            do(sq, s - 0, 0)
            do(mm2, s - 4, 0)
            do(z, s - 2, 3)
            do(zt, s - 2, 0)
            do(negm, s - 1, 3)
            do(negm, s - 0, 0)
            do(hc, s + 3, 1)
            do(sq, s - 0, 1)
            do(t1, s - 0, 2)
            do(ff, s + 2, 0)
            do(zt, s - 2, 1)
            do(yt, s + 1, 1)
            do(ff, s + 2, 1)
            do(ob, s - 5, 1)
            do(ht, s + 4, 0)
            do(t1, s - 0, 3)
            do(zt, s - 2, 2)
            do(ff, s + 2, 2)
            do(ht, s + 4, 1)
            do(yt, s + 1, 2)
            do(zt, s - 2, 3)
            do(negm, s - 0, 1)
            do(yt, s + 1, 3)
            do(ff, s + 2, 3)
            do(sq, s - 0, 2)
            do(aff, s - 2, 0)
            do(t1, s + 1, 0)
            do(z, s - 1, 0)
            do(hq, s + 3, 0)
            do(z, s - 1, 1)
            do(sq, s - 0, 3)
            do(aff, s - 2, 1)
            do(mm2, s - 4, 1)
            do(mm1, s + 3, 0)
            do(hc, s + 4, 0)
            do(z, s - 1, 2)
